import numpy as np
import ml_dtypes


def mxq(x, axis, fmt="e4m3"):
    dtype, down = {"e4m3": (ml_dtypes.float8_e4m3fn, 7), "e5m2": (ml_dtypes.float8_e5m2, 14)}[fmt]
    v = np.moveaxis(np.asarray(x, np.float32).astype(ml_dtypes.bfloat16).astype(np.float64), axis, -1)
    blocks = v.reshape(v.shape[:-1] + (-1, 32))
    amax = np.abs(blocks).max(-1, keepdims=True)
    byte = np.maximum(np.where(amax > 0, np.frexp(amax)[1] - 1 + 127, 0) - down, 1)
    scale = np.exp2(byte - 127.0)
    codes = (blocks / scale).astype(np.float32).astype(dtype).astype(np.float64)
    return np.moveaxis((codes * scale).reshape(v.shape), -1, axis)


WIDE = False


def mx_kscale(k):
    if not WIDE:
        return np.ones(k)
    levels = np.array([10, -10, 5, -5, 0])
    a = np.random.permutation(np.resize(levels, k // 512 * 4)).reshape(k // 512, 4)
    idx = np.arange(k)
    return np.exp2(a[idx // 512, idx % 128 // 32])


BF16 = ml_dtypes.bfloat16


def bf(x):
    return np.asarray(x, np.float32).astype(BF16)


def f64(x):
    return np.asarray(x).astype(np.float64)


B, S, D, H, DH = 2, 4096, 512, 2, 64
E = H * DH
EPS = 1e-12


def rotate_half(t):
    t1, t2 = np.split(t, 2, axis=-1)
    return np.concatenate((-t2, t1), axis=-1)


def apply_rotary(pos, t):
    return t * np.cos(pos) + rotate_half(t) * np.sin(pos)


def setup_inputs():
    s = mx_kscale(D)
    ang = np.random.uniform(-np.pi, np.pi, (S, DH // 2))
    col = np.concatenate((np.full(E, np.sqrt(3.0 / DH)), np.full(E, np.sqrt(3.0 / DH)), np.ones(E)))
    return {"x": bf(np.random.standard_normal((B, S, D))),
            "rotary_emb": bf(np.concatenate((ang, ang), axis=-1)),
            "gamma": bf((1.0 + 0.1 * np.random.standard_normal(D)) * s),
            "w_qkv": bf(np.random.standard_normal((D, 3 * E)) * col / np.sqrt(D) / s[:, None])}


def reference(x, rotary_emb, gamma, w_qkv):
    x, pos = f64(x), f64(rotary_emb)
    l2 = np.sqrt((x * x).sum(-1, keepdims=True))
    xn = x / np.maximum(l2, EPS) * np.sqrt(D) * f64(gamma)
    qkv = mxq(xn, 2, "e4m3") @ mxq(f64(w_qkv), 0, "e4m3")
    qkv = qkv.reshape(B, S, 3, H, DH).transpose(2, 0, 3, 1, 4)
    q, k, v = qkv[0], qkv[1], qkv[2]
    q = apply_rotary(pos, q)
    k = apply_rotary(pos, k)
    q = q * np.sqrt(DH)
    return q, k, v

@@ -1,0 +1,264 @@
+import math
+from contextlib import ExitStack
+
+import concourse.mybir as mybir
+from concourse.masks import make_identity
+
+F32 = mybir.dt.float32
+BF16 = mybir.dt.bfloat16
+U32 = mybir.dt.uint32
+U8 = mybir.dt.uint8
+FP8X4 = mybir.dt.float8_e4m3fn_x4
+ALU = mybir.AluOpType
+ACT = mybir.ActivationFunctionType
+
+P = 128
+BATCH, SEQ, DIM = 2, 4096, 512
+HEADS, HEAD_DIM = 2, 64
+HALF = HEAD_DIM // 2
+INNER = HEADS * HEAD_DIM
+PACK = 4
+POS_PER_PART = SEQ // P
+GROUP = 4
+GROUPS_PER_BATCH = POS_PER_PART // GROUP
+N_GROUPS = BATCH * GROUPS_PER_BATCH
+ROT_COLS = 4 * INNER
+EPS = 1e-12
+
+FLOPS = 2 * BATCH * SEQ * DIM * 3 * INNER
+
+
+def tile_ringattention_pa_t_kernel(tc, x, rotary_emb, gamma, w_qkv, out_0, out_1, out_2):
+    nc = tc.nc
+    x_rows = x.rearrange("b (p t) k -> b p t k", t=POS_PER_PART)
+    angle_rows = rotary_emb.rearrange("(p t) d -> p t d", t=POS_PER_PART)
+    q_rows = out_0.rearrange("b h (p t) d -> b p h t d", t=POS_PER_PART)
+    k_rows = out_1.rearrange("b h (p t) d -> b p h t d", t=POS_PER_PART)
+    v_rows = out_2.rearrange("b h (p t) d -> b p h t d", t=POS_PER_PART)
+
+    with ExitStack() as stack:
+        keep = stack.enter_context(tc.tile_pool(name="keep", bufs=1))
+        small = stack.enter_context(tc.tile_pool(name="small", bufs=4))
+        work = stack.enter_context(tc.tile_pool(name="work", bufs=2))
+        results = stack.enter_context(tc.tile_pool(name="results", bufs=3))
+        psum_keep = stack.enter_context(tc.psum_pool(name="psum_keep", bufs=1))
+        psum_t = stack.enter_context(tc.psum_pool(name="psum_t", bufs=2))
+        psum_rot = stack.enter_context(tc.psum_pool(name="psum_rot", bufs=4))
+        psum_v = stack.enter_context(tc.psum_pool(name="psum_v", bufs=1))
+
+        def where(g):
+            b, c = divmod(g, GROUPS_PER_BATCH)
+            return b, c * GROUP
+
+        gamma_row = keep.tile([P, DIM], BF16)
+        nc.vector.memset(gamma_row[:], 0.0)
+        nc.sync.dma_start(out=gamma_row[0:1, :], in_=gamma.rearrange("(o k) -> o k", o=1))
+
+        x_all = keep.tile([P, BATCH, POS_PER_PART, DIM], BF16)
+
+        def load_x(g):
+            b, t0 = where(g)
+            nc.sync.dma_start(out=x_all[:, b, t0 : t0 + GROUP, :], in_=x_rows[b, :, t0 : t0 + GROUP, :])
+
+        load_x(0)
+        w_raw = keep.tile([P, PACK, 3 * INNER], BF16)
+        nc.sync.dma_start(
+            out=w_raw[:].rearrange("p (u e) n -> p u (e n)", u=2),
+            in_=w_qkv.rearrange("(u p e) n -> p u (e n)", u=2, e=2),
+        )
+        angles = keep.tile([P, POS_PER_PART, HEAD_DIM], BF16)
+        nc.sync.dma_start(out=angles[:], in_=angle_rows)
+        for g in range(1, N_GROUPS):
+            load_x(g)
+
+        ident = keep.tile([P, P], F32)
+        make_identity(nc, ident[:])
+        minus_half = keep.tile([P, GROUP], F32)
+        nc.gpsimd.memset(minus_half[:], -0.5)
+        ones = keep.tile([P, P], BF16)
+        nc.vector.memset(ones[:], 1.0)
+        gamma_all = psum_keep.tile([P, DIM], F32)
+        nc.tensor.matmul(out=gamma_all[:], lhsT=ones[:], rhs=gamma_row[:], start=True, stop=True)
+
+        w_grouped = keep.tile([P, ROT_COLS + INNER, PACK], BF16, align_bytes=64)
+        nc.vector.tensor_copy(
+            out=w_grouped[:, 0 : 2 * INNER, :], in_=w_raw[:, :, 0 : 2 * INNER].rearrange("p j n -> p n j")
+        )
+        swapped = w_grouped[:, 2 * INNER : ROT_COLS, :].rearrange("p (g f i) j -> p g f i j", f=2, i=HALF)
+        plain = w_raw[:, :, 0 : 2 * INNER].rearrange("p j (g f i) -> p g f i j", f=2, i=HALF)
+        for f in range(2):
+            nc.vector.tensor_copy(out=swapped[:, :, f, :, :], in_=plain[:, :, 1 - f, :, :])
+        nc.vector.tensor_copy(
+            out=w_grouped[:, ROT_COLS:, :], in_=w_raw[:, :, 2 * INNER :].rearrange("p j n -> p n j")
+        )
+        w_codes = keep.tile([P, ROT_COLS + INNER], U32, align_bytes=64)
+        w_scales = keep.tile([P, ROT_COLS + INNER], U8, align_bytes=64)
+        nc.vector.quantize_mx(
+            out=w_codes[:, 0:ROT_COLS].bitcast(FP8X4),
+            scales=w_scales[:, 0:ROT_COLS],
+            in_=w_grouped[:, 0:ROT_COLS, :].rearrange("p n j -> p (n j)"),
+        )
+        nc.vector.quantize_mx(
+            out=w_codes[:, ROT_COLS:].bitcast(FP8X4),
+            scales=w_scales[:, ROT_COLS:],
+            in_=w_grouped[:, ROT_COLS:, :].rearrange("p n j -> p (n j)"),
+        )
+
+        flat_angles = angles[:].rearrange("p t d -> p (t d)")
+        minus_abs = keep.tile([P, POS_PER_PART * HEAD_DIM], BF16)
+        nc.vector.scalar_tensor_tensor(
+            out=minus_abs[:], in0=flat_angles, scalar=-1.0, in1=flat_angles, op0=ALU.mult, op1=ALU.min
+        )
+        cos_angles = keep.tile([P, POS_PER_PART, HEAD_DIM], F32)
+        nc.vector.tensor_scalar_add(
+            out=cos_angles[:].rearrange("p t d -> p (t d)"), in0=minus_abs[:], scalar1=math.pi / 2
+        )
+        table = keep.tile([P, POS_PER_PART, 2, 2, HEAD_DIM], F32)
+
+        rinv_of = {}
+        grouped_of = {}
+        operand_of = {}
+        banks_of = {}
+
+        def sums(g):
+            b, t0 = where(g)
+            mean_sq = small.tile([P, GROUP], F32)
+            for i in range(GROUP):
+                junk = small.tile([P, DIM], BF16)
+                nc.scalar.activation(
+                    out=junk[:],
+                    in_=x_all[:, b, t0 + i, :],
+                    func=ACT.Square,
+                    scale=1.0 / math.sqrt(DIM),
+                    accum_out=mean_sq[:, i : i + 1],
+                )
+            floored = small.tile([P, GROUP], F32)
+            nc.gpsimd.tensor_scalar_max(out=floored[:], in0=mean_sq[:], scalar1=EPS * EPS / DIM)
+            rinv = small.tile([P, GROUP], F32)
+            nc.gpsimd.tensor_tensor(out=rinv[:], in0=floored[:], in1=minus_half[:], op=ALU.pow)
+            rinv_of[g] = rinv
+
+        def fill_table(g):
+            t0 = g * GROUP
+            ts = slice(t0, t0 + GROUP)
+            nc.scalar.activation(out=table[:, ts, 0, 1, :], in_=cos_angles[:, ts, :], func=ACT.Sin)
+            nc.scalar.activation(
+                out=table[:, ts, 1, 1, 0:HALF], in_=angles[:, ts, 0:HALF], func=ACT.Sin, scale=-1.0
+            )
+            nc.scalar.activation(out=table[:, ts, 1, 1, HALF:], in_=angles[:, ts, HALF:], func=ACT.Sin)
+            nc.gpsimd.tensor_scalar(
+                out=table[:, ts, :, 0, :],
+                in0=table[:, ts, :, 1, :],
+                scalar1=math.sqrt(HEAD_DIM),
+                scalar2=0.0,
+                op0=ALU.mult,
+                op1=ALU.add,
+            )
+
+        def normalise(g):
+            b, t0 = where(g)
+            rinv = rinv_of.pop(g)
+            xn = work.tile([P, GROUP, DIM], BF16)
+            for i in range(GROUP):
+                nc.vector.scalar_tensor_tensor(
+                    out=xn[:, i, :],
+                    in0=x_all[:, b, t0 + i, :],
+                    scalar=rinv[:, i : i + 1],
+                    in1=gamma_all[:],
+                    op0=ALU.mult,
+                    op1=ALU.mult,
+                )
+            xn_words = xn[:].bitcast(F32)
+            grouped = work.tile([P, GROUP, P, PACK], BF16, align_bytes=64)
+            grouped_words = grouped[:].bitcast(F32)
+            for h in range(GROUP // 2):
+                xt = psum_t.tile([P, 2, 2, P], F32)
+                for i in range(2):
+                    for u in range(2):
+                        nc.tensor.transpose(xt[:, i, u, :], xn_words[:, 2 * h + i, u * P : (u + 1) * P], ident[:])
+                nc.scalar.copy(
+                    out=grouped_words[:, 2 * h : 2 * h + 2, :, :], in_=xt[:].rearrange("p i u r -> p i r u")
+                )
+            grouped_of[g] = grouped
+
+        def quantise(g):
+            grouped = grouped_of.pop(g)
+            codes = work.tile([P, GROUP * P], U32, align_bytes=64)
+            scales = work.tile([P, GROUP * P], U8, align_bytes=64)
+            nc.vector.quantize_mx(
+                out=codes[:].bitcast(FP8X4), scales=scales[:], in_=grouped[:].rearrange("p i r j -> p (i r j)")
+            )
+            operand_of[g] = (codes, scales)
+
+        def project(g):
+            codes, scales = operand_of.pop(g)
+            v_bank = psum_v.tile([P, GROUP, INNER], F32)
+            rot_banks = []
+            for i in range(GROUP):
+                rows = slice(i * P, (i + 1) * P)
+                rot_bank = psum_rot.tile([P, ROT_COLS], F32)
+                nc.tensor.matmul_mx(
+                    out=rot_bank[:],
+                    lhsT=codes[:, rows].bitcast(FP8X4),
+                    lhsT_scale=scales[:, rows],
+                    rhs=w_codes[:, 0:ROT_COLS].bitcast(FP8X4),
+                    rhs_scale=w_scales[:, 0:ROT_COLS],
+                    start=True,
+                    stop=True,
+                )
+                nc.tensor.matmul_mx(
+                    out=v_bank[:, i, :],
+                    lhsT=codes[:, rows].bitcast(FP8X4),
+                    lhsT_scale=scales[:, rows],
+                    rhs=w_codes[:, ROT_COLS:].bitcast(FP8X4),
+                    rhs_scale=w_scales[:, ROT_COLS:],
+                    start=True,
+                    stop=True,
+                )
+                rot_banks.append(rot_bank)
+            banks_of[g] = (rot_banks, v_bank)
+
+        def rotate(g):
+            b, t0 = where(g)
+            rot_banks, v_bank = banks_of.pop(g)
+            v_out = results.tile([P, HEADS, GROUP, HEAD_DIM], F32)
+            nc.scalar.copy(
+                out=v_out[:].rearrange("p h i d -> p i h d"),
+                in_=v_bank[:].rearrange("p i (h d) -> p i h d", h=HEADS),
+            )
+            nc.sync.dma_start(out=v_rows[b, :, :, t0 : t0 + GROUP, :], in_=v_out[:])
+            products = work.tile([P, GROUP, ROT_COLS], F32)
+            for i in range(GROUP):
+                factors = table[:, t0 + i, :, :, :].rearrange("p c q d -> p (c q) d").unsqueeze(2)
+                nc.vector.tensor_tensor(
+                    out=products[:, i, :].rearrange("p (c h d) -> p c h d", h=HEADS, d=HEAD_DIM),
+                    in0=rot_banks[i][:].rearrange("p (c h d) -> p c h d", h=HEADS, d=HEAD_DIM),
+                    in1=factors.to_broadcast([P, 4, HEADS, HEAD_DIM]),
+                    op=ALU.mult,
+                )
+            qk_out = results.tile([P, 2 * HEADS, GROUP, HEAD_DIM], F32)
+            nc.gpsimd.tensor_tensor(
+                out=qk_out[:].rearrange("p g i d -> p i g d"),
+                in0=products[:, :, 0 : 2 * INNER].rearrange("p i (g d) -> p i g d", d=HEAD_DIM),
+                in1=products[:, :, 2 * INNER :].rearrange("p i (g d) -> p i g d", d=HEAD_DIM),
+                op=ALU.add,
+            )
+            nc.sync.dma_start(out=q_rows[b, :, :, t0 : t0 + GROUP, :], in_=qk_out[:, 0:HEADS, :, :])
+            nc.sync.dma_start(out=k_rows[b, :, :, t0 : t0 + GROUP, :], in_=qk_out[:, HEADS:, :, :])
+
+        sums(0)
+        sums(1)
+        fill_table(0)
+        normalise(0)
+        quantise(0)
+        for g in range(N_GROUPS):
+            if g + 2 < N_GROUPS:
+                sums(g + 2)
+            if g + 1 < GROUPS_PER_BATCH:
+                fill_table(g + 1)
+            project(g)
+            if g + 1 < N_GROUPS:
+                normalise(g + 1)
+            rotate(g)
+            if g + 1 < N_GROUPS:
+                quantise(g + 1)

@@ -38,13 +38,14 @@ def tile_ringattention_pa_t_kernel(tc, x, rotary_emb, gamma, w_qkv, out_0, out_1
 
     with ExitStack() as stack:
         keep = stack.enter_context(tc.tile_pool(name="keep", bufs=1))
-        small = stack.enter_context(tc.tile_pool(name="small", bufs=4))
+        small = stack.enter_context(tc.tile_pool(name="small", bufs=6))
         work = stack.enter_context(tc.tile_pool(name="work", bufs=2))
         results = stack.enter_context(tc.tile_pool(name="results", bufs=3))
         psum_keep = stack.enter_context(tc.psum_pool(name="psum_keep", bufs=1))
         psum_t = stack.enter_context(tc.psum_pool(name="psum_t", bufs=2))
         psum_rot = stack.enter_context(tc.psum_pool(name="psum_rot", bufs=4))
         psum_v = stack.enter_context(tc.psum_pool(name="psum_v", bufs=1))
+        stack.enter_context(tc.manual_schedule())
 
         def where(g):
             b, c = divmod(g, GROUPS_PER_BATCH)
@@ -119,6 +120,9 @@ def tile_ringattention_pa_t_kernel(tc, x, rotary_emb, gamma, w_qkv, out_0, out_1
         grouped_of = {}
         operand_of = {}
         banks_of = {}
+        v_bank_of = {}
+        transposed_of = {}
+        products_of = {}
 
         def sums(g):
             b, t0 = where(g)
@@ -169,15 +173,22 @@ def tile_ringattention_pa_t_kernel(tc, x, rotary_emb, gamma, w_qkv, out_0, out_1
                     op1=ALU.mult,
                 )
             xn_words = xn[:].bitcast(F32)
-            grouped = work.tile([P, GROUP, P, PACK], BF16, align_bytes=64)
-            grouped_words = grouped[:].bitcast(F32)
+            pairs = []
             for h in range(GROUP // 2):
                 xt = psum_t.tile([P, 2, 2, P], F32)
                 for i in range(2):
                     for u in range(2):
                         nc.tensor.transpose(xt[:, i, u, :], xn_words[:, 2 * h + i, u * P : (u + 1) * P], ident[:])
+                pairs.append(xt)
+            transposed_of[g] = pairs
+
+        def regroup(g):
+            pairs = transposed_of.pop(g)
+            grouped = work.tile([P, GROUP, P, PACK], BF16, align_bytes=64)
+            grouped_words = grouped[:].bitcast(F32)
+            for h in range(GROUP // 2):
                 nc.scalar.copy(
-                    out=grouped_words[:, 2 * h : 2 * h + 2, :, :], in_=xt[:].rearrange("p i u r -> p i r u")
+                    out=grouped_words[:, 2 * h : 2 * h + 2, :, :], in_=pairs[h][:].rearrange("p i u r -> p i r u")
                 )
             grouped_of[g] = grouped
 
@@ -216,17 +227,22 @@ def tile_ringattention_pa_t_kernel(tc, x, rotary_emb, gamma, w_qkv, out_0, out_1
                     stop=True,
                 )
                 rot_banks.append(rot_bank)
-            banks_of[g] = (rot_banks, v_bank)
+            banks_of[g] = rot_banks
+            v_bank_of[g] = v_bank
 
-        def rotate(g):
+        def copy_v(g):
             b, t0 = where(g)
-            rot_banks, v_bank = banks_of.pop(g)
+            v_bank = v_bank_of.pop(g)
             v_out = results.tile([P, HEADS, GROUP, HEAD_DIM], F32)
             nc.scalar.copy(
                 out=v_out[:].rearrange("p h i d -> p i h d"),
                 in_=v_bank[:].rearrange("p i (h d) -> p i h d", h=HEADS),
             )
             nc.sync.dma_start(out=v_rows[b, :, :, t0 : t0 + GROUP, :], in_=v_out[:])
+
+        def rotate(g):
+            b, t0 = where(g)
+            rot_banks = banks_of.pop(g)
             products = work.tile([P, GROUP, ROT_COLS], F32)
             for i in range(GROUP):
                 factors = table[:, t0 + i, :, :, :].rearrange("p c q d -> p (c q) d").unsqueeze(2)
@@ -236,6 +252,11 @@ def tile_ringattention_pa_t_kernel(tc, x, rotary_emb, gamma, w_qkv, out_0, out_1
                     in1=factors.to_broadcast([P, 4, HEADS, HEAD_DIM]),
                     op=ALU.mult,
                 )
+            products_of[g] = products
+
+        def add_and_store(g):
+            b, t0 = where(g)
+            products = products_of.pop(g)
             qk_out = results.tile([P, 2 * HEADS, GROUP, HEAD_DIM], F32)
             nc.gpsimd.tensor_tensor(
                 out=qk_out[:].rearrange("p g i d -> p i g d"),
@@ -246,19 +267,17 @@ def tile_ringattention_pa_t_kernel(tc, x, rotary_emb, gamma, w_qkv, out_0, out_1
             nc.sync.dma_start(out=q_rows[b, :, :, t0 : t0 + GROUP, :], in_=qk_out[:, 0:HEADS, :, :])
             nc.sync.dma_start(out=k_rows[b, :, :, t0 : t0 + GROUP, :], in_=qk_out[:, HEADS:, :, :])
 
-        sums(0)
-        sums(1)
-        fill_table(0)
-        normalise(0)
-        quantise(0)
-        for g in range(N_GROUPS):
-            if g + 2 < N_GROUPS:
-                sums(g + 2)
-            if g + 1 < GROUPS_PER_BATCH:
-                fill_table(g + 1)
-            project(g)
-            if g + 1 < N_GROUPS:
-                normalise(g + 1)
-            rotate(g)
-            if g + 1 < N_GROUPS:
-                quantise(g + 1)
+        def run(stage, g, groups=N_GROUPS):
+            if 0 <= g < groups:
+                stage(g)
+
+        for g in range(-4, N_GROUPS + 1):
+            run(project, g)
+            run(normalise, g + 2)
+            run(add_and_store, g - 1)
+            run(sums, g + 4)
+            run(copy_v, g)
+            run(regroup, g + 2)
+            run(fill_table, g + 2, GROUPS_PER_BATCH)
+            run(rotate, g)
+            run(quantise, g + 1)

@@ -48,7 +48,7 @@ def tile_ringattention_pa_t_kernel(tc, x, rotary_emb, gamma, w_qkv, out_0, out_1
         stack.enter_context(tc.manual_schedule())
 
         def where(g):
-            b, c = divmod(g, GROUPS_PER_BATCH)
+            c, b = divmod(g, BATCH)
             return b, c * GROUP
 
         gamma_row = keep.tile([P, DIM], BF16)
@@ -80,6 +80,9 @@ def tile_ringattention_pa_t_kernel(tc, x, rotary_emb, gamma, w_qkv, out_0, out_1
         nc.vector.memset(ones[:], 1.0)
         gamma_all = psum_keep.tile([P, DIM], F32)
         nc.tensor.matmul(out=gamma_all[:], lhsT=ones[:], rhs=gamma_row[:], start=True, stop=True)
+
+        gamma_sbuf = keep.tile([P, DIM], F32)
+        nc.scalar.copy(out=gamma_sbuf[:], in_=gamma_all[:])
 
         w_grouped = keep.tile([P, ROT_COLS + INNER, PACK], BF16, align_bytes=64)
         nc.vector.tensor_copy(
@@ -123,6 +126,7 @@ def tile_ringattention_pa_t_kernel(tc, x, rotary_emb, gamma, w_qkv, out_0, out_1
         v_bank_of = {}
         transposed_of = {}
         products_of = {}
+        x_gamma_of = {}
 
         def sums(g):
             b, t0 = where(g)
@@ -143,7 +147,9 @@ def tile_ringattention_pa_t_kernel(tc, x, rotary_emb, gamma, w_qkv, out_0, out_1
             rinv_of[g] = rinv
 
         def fill_table(g):
-            t0 = g * GROUP
+            b, t0 = where(g)
+            if b > 0:
+                return
             ts = slice(t0, t0 + GROUP)
             nc.scalar.activation(out=table[:, ts, 0, 1, :], in_=cos_angles[:, ts, :], func=ACT.Sin)
             nc.scalar.activation(
@@ -159,11 +165,25 @@ def tile_ringattention_pa_t_kernel(tc, x, rotary_emb, gamma, w_qkv, out_0, out_1
                 op1=ALU.add,
             )
 
+        def premultiply(g):
+            b, t0 = where(g)
+            x_gamma = small.tile([P, DIM], F32)
+            nc.gpsimd.tensor_tensor(
+                out=x_gamma[:], in0=x_all[:, b, t0 + GROUP - 1, :], in1=gamma_sbuf[:], op=ALU.mult
+            )
+            x_gamma_of[g] = x_gamma
+
         def normalise(g):
             b, t0 = where(g)
             rinv = rinv_of.pop(g)
             xn = work.tile([P, GROUP, DIM], BF16)
-            for i in range(GROUP):
+            nc.scalar.activation(
+                out=xn[:, GROUP - 1, :],
+                in_=x_gamma_of.pop(g)[:],
+                func=ACT.Copy,
+                scale=rinv[:, GROUP - 1 : GROUP],
+            )
+            for i in range(GROUP - 1):
                 nc.vector.scalar_tensor_tensor(
                     out=xn[:, i, :],
                     in0=x_all[:, b, t0 + i, :],
@@ -267,17 +287,18 @@ def tile_ringattention_pa_t_kernel(tc, x, rotary_emb, gamma, w_qkv, out_0, out_1
             nc.sync.dma_start(out=q_rows[b, :, :, t0 : t0 + GROUP, :], in_=qk_out[:, 0:HEADS, :, :])
             nc.sync.dma_start(out=k_rows[b, :, :, t0 : t0 + GROUP, :], in_=qk_out[:, HEADS:, :, :])
 
-        def run(stage, g, groups=N_GROUPS):
-            if 0 <= g < groups:
+        def run(stage, g):
+            if 0 <= g < N_GROUPS:
                 stage(g)
 
         for g in range(-4, N_GROUPS + 1):
             run(project, g)
             run(normalise, g + 2)
             run(add_and_store, g - 1)
+            run(premultiply, g + 3)
             run(sums, g + 4)
             run(copy_v, g)
             run(regroup, g + 2)
-            run(fill_table, g + 2, GROUPS_PER_BATCH)
+            run(fill_table, g + 2)
             run(rotate, g)
             run(quantise, g + 1)

@@ -59,7 +59,8 @@ def tile_ringattention_pa_t_kernel(tc, x, rotary_emb, gamma, w_qkv, out_0, out_1
 
         def load_x(g):
             b, t0 = where(g)
-            nc.sync.dma_start(out=x_all[:, b, t0 : t0 + GROUP, :], in_=x_rows[b, :, t0 : t0 + GROUP, :])
+            for t in range(t0, t0 + GROUP, 2):
+                nc.sync.dma_start(out=x_all[:, b, t : t + 2, :], in_=x_rows[b, :, t : t + 2, :])
 
         load_x(0)
         w_raw = keep.tile([P, PACK, 3 * INNER], BF16)
@@ -80,9 +81,6 @@ def tile_ringattention_pa_t_kernel(tc, x, rotary_emb, gamma, w_qkv, out_0, out_1
         nc.vector.memset(ones[:], 1.0)
         gamma_all = psum_keep.tile([P, DIM], F32)
         nc.tensor.matmul(out=gamma_all[:], lhsT=ones[:], rhs=gamma_row[:], start=True, stop=True)
-
-        gamma_sbuf = keep.tile([P, DIM], F32)
-        nc.scalar.copy(out=gamma_sbuf[:], in_=gamma_all[:])
 
         w_grouped = keep.tile([P, ROT_COLS + INNER, PACK], BF16, align_bytes=64)
         nc.vector.tensor_copy(
@@ -108,15 +106,6 @@ def tile_ringattention_pa_t_kernel(tc, x, rotary_emb, gamma, w_qkv, out_0, out_1
             in_=w_grouped[:, ROT_COLS:, :].rearrange("p n j -> p (n j)"),
         )
 
-        flat_angles = angles[:].rearrange("p t d -> p (t d)")
-        minus_abs = keep.tile([P, POS_PER_PART * HEAD_DIM], BF16)
-        nc.vector.scalar_tensor_tensor(
-            out=minus_abs[:], in0=flat_angles, scalar=-1.0, in1=flat_angles, op0=ALU.mult, op1=ALU.min
-        )
-        cos_angles = keep.tile([P, POS_PER_PART, HEAD_DIM], F32)
-        nc.vector.tensor_scalar_add(
-            out=cos_angles[:].rearrange("p t d -> p (t d)"), in0=minus_abs[:], scalar1=math.pi / 2
-        )
         table = keep.tile([P, POS_PER_PART, 2, 2, HEAD_DIM], F32)
 
         rinv_of = {}
@@ -126,7 +115,6 @@ def tile_ringattention_pa_t_kernel(tc, x, rotary_emb, gamma, w_qkv, out_0, out_1
         v_bank_of = {}
         transposed_of = {}
         products_of = {}
-        x_gamma_of = {}
 
         def sums(g):
             b, t0 = where(g)
@@ -151,11 +139,15 @@ def tile_ringattention_pa_t_kernel(tc, x, rotary_emb, gamma, w_qkv, out_0, out_1
             if b > 0:
                 return
             ts = slice(t0, t0 + GROUP)
-            nc.scalar.activation(out=table[:, ts, 0, 1, :], in_=cos_angles[:, ts, :], func=ACT.Sin)
+            half_sin = small.tile([P, GROUP, HEAD_DIM], F32)
+            nc.scalar.activation(out=half_sin[:], in_=angles[:, ts, :], func=ACT.Sin, scale=0.5)
             nc.scalar.activation(
                 out=table[:, ts, 1, 1, 0:HALF], in_=angles[:, ts, 0:HALF], func=ACT.Sin, scale=-1.0
             )
+            twice_sq = small.tile([P, GROUP, HEAD_DIM], F32)
+            nc.scalar.activation(out=twice_sq[:], in_=half_sin[:], func=ACT.Square, scale=math.sqrt(2.0))
             nc.scalar.activation(out=table[:, ts, 1, 1, HALF:], in_=angles[:, ts, HALF:], func=ACT.Sin)
+            nc.scalar.activation(out=table[:, ts, 0, 1, :], in_=twice_sq[:], func=ACT.Copy, scale=-1.0, bias=1.0)
             nc.gpsimd.tensor_scalar(
                 out=table[:, ts, :, 0, :],
                 in0=table[:, ts, :, 1, :],
@@ -165,25 +157,11 @@ def tile_ringattention_pa_t_kernel(tc, x, rotary_emb, gamma, w_qkv, out_0, out_1
                 op1=ALU.add,
             )
 
-        def premultiply(g):
-            b, t0 = where(g)
-            x_gamma = small.tile([P, DIM], F32)
-            nc.gpsimd.tensor_tensor(
-                out=x_gamma[:], in0=x_all[:, b, t0 + GROUP - 1, :], in1=gamma_sbuf[:], op=ALU.mult
-            )
-            x_gamma_of[g] = x_gamma
-
         def normalise(g):
             b, t0 = where(g)
             rinv = rinv_of.pop(g)
             xn = work.tile([P, GROUP, DIM], BF16)
-            nc.scalar.activation(
-                out=xn[:, GROUP - 1, :],
-                in_=x_gamma_of.pop(g)[:],
-                func=ACT.Copy,
-                scale=rinv[:, GROUP - 1 : GROUP],
-            )
-            for i in range(GROUP - 1):
+            for i in range(GROUP):
                 nc.vector.scalar_tensor_tensor(
                     out=xn[:, i, :],
                     in0=x_all[:, b, t0 + i, :],
@@ -278,7 +256,8 @@ def tile_ringattention_pa_t_kernel(tc, x, rotary_emb, gamma, w_qkv, out_0, out_1
             b, t0 = where(g)
             products = products_of.pop(g)
             qk_out = results.tile([P, 2 * HEADS, GROUP, HEAD_DIM], F32)
-            nc.gpsimd.tensor_tensor(
+            adder = nc.vector if g == N_GROUPS - 1 else nc.gpsimd
+            adder.tensor_tensor(
                 out=qk_out[:].rearrange("p g i d -> p i g d"),
                 in0=products[:, :, 0 : 2 * INNER].rearrange("p i (g d) -> p i g d", d=HEAD_DIM),
                 in1=products[:, :, 2 * INNER :].rearrange("p i (g d) -> p i g d", d=HEAD_DIM),
@@ -295,7 +274,6 @@ def tile_ringattention_pa_t_kernel(tc, x, rotary_emb, gamma, w_qkv, out_0, out_1
             run(project, g)
             run(normalise, g + 2)
             run(add_and_store, g - 1)
-            run(premultiply, g + 3)
             run(sums, g + 4)
             run(copy_v, g)
             run(regroup, g + 2)

@@ -51,10 +51,6 @@ def tile_ringattention_pa_t_kernel(tc, x, rotary_emb, gamma, w_qkv, out_0, out_1
             c, b = divmod(g, BATCH)
             return b, c * GROUP
 
-        gamma_row = keep.tile([P, DIM], BF16)
-        nc.vector.memset(gamma_row[:], 0.0)
-        nc.sync.dma_start(out=gamma_row[0:1, :], in_=gamma.rearrange("(o k) -> o k", o=1))
-
         x_all = keep.tile([P, BATCH, POS_PER_PART, DIM], BF16)
 
         def load_x(g):
@@ -63,14 +59,18 @@ def tile_ringattention_pa_t_kernel(tc, x, rotary_emb, gamma, w_qkv, out_0, out_1
                 nc.sync.dma_start(out=x_all[:, b, t : t + 2, :], in_=x_rows[b, :, t : t + 2, :])
 
         load_x(0)
+        gamma_row = keep.tile([P, DIM], BF16)
+        nc.vector.memset(gamma_row[:], 0.0)
+        nc.sync.dma_start(out=gamma_row[0:1, :], in_=gamma.rearrange("(o k) -> o k", o=1))
         w_raw = keep.tile([P, PACK, 3 * INNER], BF16)
         nc.sync.dma_start(
             out=w_raw[:].rearrange("p (u e) n -> p u (e n)", u=2),
             in_=w_qkv.rearrange("(u p e) n -> p u (e n)", u=2, e=2),
         )
+        load_x(1)
         angles = keep.tile([P, POS_PER_PART, HEAD_DIM], BF16)
         nc.sync.dma_start(out=angles[:], in_=angle_rows)
-        for g in range(1, N_GROUPS):
+        for g in range(2, N_GROUPS):
             load_x(g)
 
         ident = keep.tile([P, P], F32)

@@ -75,8 +75,11 @@ def tile_ringattention_pa_t_kernel(tc, x, rotary_emb, gamma, w_qkv, out_0, out_1
 
         ident = keep.tile([P, P], F32)
         make_identity(nc, ident[:])
-        minus_half = keep.tile([P, GROUP], F32)
+        minus_half = keep.tile([P, 2 * GROUP], F32)
         nc.gpsimd.memset(minus_half[:], -0.5)
+        mean_sq = keep.tile([P, N_GROUPS * GROUP], F32)
+        floored = keep.tile([P, N_GROUPS * GROUP], F32)
+        rinv = keep.tile([P, N_GROUPS * GROUP], F32)
         ones = keep.tile([P, P], BF16)
         nc.vector.memset(ones[:], 1.0)
         gamma_all = psum_keep.tile([P, DIM], F32)
@@ -108,7 +111,6 @@ def tile_ringattention_pa_t_kernel(tc, x, rotary_emb, gamma, w_qkv, out_0, out_1
 
         table = keep.tile([P, POS_PER_PART, 2, 2, HEAD_DIM], F32)
 
-        rinv_of = {}
         grouped_of = {}
         operand_of = {}
         banks_of = {}
@@ -118,7 +120,6 @@ def tile_ringattention_pa_t_kernel(tc, x, rotary_emb, gamma, w_qkv, out_0, out_1
 
         def sums(g):
             b, t0 = where(g)
-            mean_sq = small.tile([P, GROUP], F32)
             for i in range(GROUP):
                 junk = small.tile([P, DIM], BF16)
                 nc.scalar.activation(
@@ -126,13 +127,18 @@ def tile_ringattention_pa_t_kernel(tc, x, rotary_emb, gamma, w_qkv, out_0, out_1
                     in_=x_all[:, b, t0 + i, :],
                     func=ACT.Square,
                     scale=1.0 / math.sqrt(DIM),
-                    accum_out=mean_sq[:, i : i + 1],
+                    accum_out=mean_sq[:, g * GROUP + i : g * GROUP + i + 1],
                 )
-            floored = small.tile([P, GROUP], F32)
-            nc.gpsimd.tensor_scalar_max(out=floored[:], in0=mean_sq[:], scalar1=EPS * EPS / DIM)
-            rinv = small.tile([P, GROUP], F32)
-            nc.gpsimd.tensor_tensor(out=rinv[:], in0=floored[:], in1=minus_half[:], op=ALU.pow)
-            rinv_of[g] = rinv
+            if g == 0 or g % 2 == 1:
+                first = g if g < 2 else g - 1
+                cols = slice(first * GROUP, (g + 1) * GROUP)
+                nc.gpsimd.tensor_scalar_max(out=floored[:, cols], in0=mean_sq[:, cols], scalar1=EPS * EPS / DIM)
+                nc.gpsimd.tensor_tensor(
+                    out=rinv[:, cols],
+                    in0=floored[:, cols],
+                    in1=minus_half[:, 0 : (g + 1 - first) * GROUP],
+                    op=ALU.pow,
+                )
 
         def fill_table(g):
             b, t0 = where(g)
@@ -159,13 +165,12 @@ def tile_ringattention_pa_t_kernel(tc, x, rotary_emb, gamma, w_qkv, out_0, out_1
 
         def normalise(g):
             b, t0 = where(g)
-            rinv = rinv_of.pop(g)
             xn = work.tile([P, GROUP, DIM], BF16)
             for i in range(GROUP):
                 nc.vector.scalar_tensor_tensor(
                     out=xn[:, i, :],
                     in0=x_all[:, b, t0 + i, :],
-                    scalar=rinv[:, i : i + 1],
+                    scalar=rinv[:, g * GROUP + i : g * GROUP + i + 1],
                     in1=gamma_all[:],
                     op0=ALU.mult,
                     op1=ALU.mult,
@@ -241,7 +246,7 @@ def tile_ringattention_pa_t_kernel(tc, x, rotary_emb, gamma, w_qkv, out_0, out_1
         def rotate(g):
             b, t0 = where(g)
             rot_banks = banks_of.pop(g)
-            products = work.tile([P, GROUP, ROT_COLS], F32)
+            products = results.tile([P, GROUP, ROT_COLS], F32)
             for i in range(GROUP):
                 factors = table[:, t0 + i, :, :, :].rearrange("p c q d -> p (c q) d").unsqueeze(2)
                 nc.vector.tensor_tensor(
@@ -270,11 +275,11 @@ def tile_ringattention_pa_t_kernel(tc, x, rotary_emb, gamma, w_qkv, out_0, out_1
             if 0 <= g < N_GROUPS:
                 stage(g)
 
-        for g in range(-4, N_GROUPS + 1):
+        for g in range(-5, N_GROUPS + 1):
             run(project, g)
             run(normalise, g + 2)
             run(add_and_store, g - 1)
-            run(sums, g + 4)
+            run(sums, g + 5)
             run(copy_v, g)
             run(regroup, g + 2)
             run(fill_table, g + 2)

import math
from contextlib import ExitStack

import concourse.mybir as mybir
from concourse.masks import make_identity

F32 = mybir.dt.float32
BF16 = mybir.dt.bfloat16
U32 = mybir.dt.uint32
U8 = mybir.dt.uint8
FP8X4 = mybir.dt.float8_e4m3fn_x4
ALU = mybir.AluOpType
ACT = mybir.ActivationFunctionType

P = 128
BATCH, SEQ, DIM = 2, 4096, 512
HEADS, HEAD_DIM = 2, 64
HALF = HEAD_DIM // 2
INNER = HEADS * HEAD_DIM
PACK = 4
POS_PER_PART = SEQ // P
GROUP = 4
GROUPS_PER_BATCH = POS_PER_PART // GROUP
N_GROUPS = BATCH * GROUPS_PER_BATCH
ROT_COLS = 4 * INNER
EPS = 1e-12

FLOPS = 2 * BATCH * SEQ * DIM * 3 * INNER


def tile_ringattention_pa_t_kernel(tc, x, rotary_emb, gamma, w_qkv, out_0, out_1, out_2):
    nc = tc.nc
    x_rows = x.rearrange("b (p t) k -> b p t k", t=POS_PER_PART)
    angle_rows = rotary_emb.rearrange("(p t) d -> p t d", t=POS_PER_PART)
    q_rows = out_0.rearrange("b h (p t) d -> b p h t d", t=POS_PER_PART)
    k_rows = out_1.rearrange("b h (p t) d -> b p h t d", t=POS_PER_PART)
    v_rows = out_2.rearrange("b h (p t) d -> b p h t d", t=POS_PER_PART)

    with ExitStack() as stack:
        keep = stack.enter_context(tc.tile_pool(name="keep", bufs=1))
        small = stack.enter_context(tc.tile_pool(name="small", bufs=6))
        work = stack.enter_context(tc.tile_pool(name="work", bufs=2))
        results = stack.enter_context(tc.tile_pool(name="results", bufs=3))
        psum_keep = stack.enter_context(tc.psum_pool(name="psum_keep", bufs=1))
        psum_t = stack.enter_context(tc.psum_pool(name="psum_t", bufs=2))
        psum_rot = stack.enter_context(tc.psum_pool(name="psum_rot", bufs=4))
        psum_v = stack.enter_context(tc.psum_pool(name="psum_v", bufs=1))
        stack.enter_context(tc.manual_schedule())

        def where(g):
            c, b = divmod(g, BATCH)
            return b, c * GROUP

        x_all = keep.tile([P, BATCH, POS_PER_PART, DIM], BF16)

        def load_x(g):
            b, t0 = where(g)
            for t in range(t0, t0 + GROUP, 2):
                nc.sync.dma_start(out=x_all[:, b, t : t + 2, :], in_=x_rows[b, :, t : t + 2, :])

        load_x(0)
        gamma_row = keep.tile([P, DIM], BF16)
        nc.vector.memset(gamma_row[:], 0.0)
        nc.sync.dma_start(out=gamma_row[0:1, :], in_=gamma.rearrange("(o k) -> o k", o=1))
        w_raw = keep.tile([P, PACK, 3 * INNER], BF16)
        nc.sync.dma_start(
            out=w_raw[:].rearrange("p (u e) n -> p u (e n)", u=2),
            in_=w_qkv.rearrange("(u p e) n -> p u (e n)", u=2, e=2),
        )
        load_x(1)
        angles = keep.tile([P, POS_PER_PART, HEAD_DIM], BF16)
        nc.sync.dma_start(out=angles[:], in_=angle_rows)
        for g in range(2, N_GROUPS):
            load_x(g)

        ident = keep.tile([P, P], F32)
        make_identity(nc, ident[:])
        minus_half = keep.tile([P, 2 * GROUP], F32)
        nc.gpsimd.memset(minus_half[:], -0.5)
        mean_sq = keep.tile([P, N_GROUPS * GROUP], F32)
        floored = keep.tile([P, N_GROUPS * GROUP], F32)
        rinv = keep.tile([P, N_GROUPS * GROUP], F32)
        ones = keep.tile([P, P], BF16)
        nc.vector.memset(ones[:], 1.0)
        gamma_all = psum_keep.tile([P, DIM], F32)
        nc.tensor.matmul(out=gamma_all[:], lhsT=ones[:], rhs=gamma_row[:], start=True, stop=True)

        w_grouped = keep.tile([P, ROT_COLS + INNER, PACK], BF16, align_bytes=64)
        nc.vector.tensor_copy(
            out=w_grouped[:, 0 : 2 * INNER, :], in_=w_raw[:, :, 0 : 2 * INNER].rearrange("p j n -> p n j")
        )
        swapped = w_grouped[:, 2 * INNER : ROT_COLS, :].rearrange("p (g f i) j -> p g f i j", f=2, i=HALF)
        plain = w_raw[:, :, 0 : 2 * INNER].rearrange("p j (g f i) -> p g f i j", f=2, i=HALF)
        for f in range(2):
            nc.vector.tensor_copy(out=swapped[:, :, f, :, :], in_=plain[:, :, 1 - f, :, :])
        nc.vector.tensor_copy(
            out=w_grouped[:, ROT_COLS:, :], in_=w_raw[:, :, 2 * INNER :].rearrange("p j n -> p n j")
        )
        w_codes = keep.tile([P, ROT_COLS + INNER], U32, align_bytes=64)
        w_scales = keep.tile([P, ROT_COLS + INNER], U8, align_bytes=64)
        nc.vector.quantize_mx(
            out=w_codes[:, 0:ROT_COLS].bitcast(FP8X4),
            scales=w_scales[:, 0:ROT_COLS],
            in_=w_grouped[:, 0:ROT_COLS, :].rearrange("p n j -> p (n j)"),
        )
        nc.vector.quantize_mx(
            out=w_codes[:, ROT_COLS:].bitcast(FP8X4),
            scales=w_scales[:, ROT_COLS:],
            in_=w_grouped[:, ROT_COLS:, :].rearrange("p n j -> p (n j)"),
        )

        table = keep.tile([P, POS_PER_PART, 2, 2, HEAD_DIM], F32)

        grouped_of = {}
        operand_of = {}
        banks_of = {}
        v_bank_of = {}
        transposed_of = {}
        products_of = {}

        def sums(g):
            b, t0 = where(g)
            for i in range(GROUP):
                junk = small.tile([P, DIM], BF16)
                nc.scalar.activation(
                    out=junk[:],
                    in_=x_all[:, b, t0 + i, :],
                    func=ACT.Square,
                    scale=1.0 / math.sqrt(DIM),
                    accum_out=mean_sq[:, g * GROUP + i : g * GROUP + i + 1],
                )
            if g == 0 or g % 2 == 1:
                first = g if g < 2 else g - 1
                cols = slice(first * GROUP, (g + 1) * GROUP)
                nc.gpsimd.tensor_scalar_max(out=floored[:, cols], in0=mean_sq[:, cols], scalar1=EPS * EPS / DIM)
                nc.gpsimd.tensor_tensor(
                    out=rinv[:, cols],
                    in0=floored[:, cols],
                    in1=minus_half[:, 0 : (g + 1 - first) * GROUP],
                    op=ALU.pow,
                )

        def fill_table(g):
            b, t0 = where(g)
            if b > 0:
                return
            ts = slice(t0, t0 + GROUP)
            half_sin = small.tile([P, GROUP, HEAD_DIM], F32)
            nc.scalar.activation(out=half_sin[:], in_=angles[:, ts, :], func=ACT.Sin, scale=0.5)
            nc.scalar.activation(
                out=table[:, ts, 1, 1, 0:HALF], in_=angles[:, ts, 0:HALF], func=ACT.Sin, scale=-1.0
            )
            twice_sq = small.tile([P, GROUP, HEAD_DIM], F32)
            nc.scalar.activation(out=twice_sq[:], in_=half_sin[:], func=ACT.Square, scale=math.sqrt(2.0))
            nc.scalar.activation(out=table[:, ts, 1, 1, HALF:], in_=angles[:, ts, HALF:], func=ACT.Sin)
            nc.scalar.activation(out=table[:, ts, 0, 1, :], in_=twice_sq[:], func=ACT.Copy, scale=-1.0, bias=1.0)
            nc.gpsimd.tensor_scalar(
                out=table[:, ts, :, 0, :],
                in0=table[:, ts, :, 1, :],
                scalar1=math.sqrt(HEAD_DIM),
                scalar2=0.0,
                op0=ALU.mult,
                op1=ALU.add,
            )

        def normalise(g):
            b, t0 = where(g)
            xn = work.tile([P, GROUP, DIM], BF16)
            for i in range(GROUP):
                nc.vector.scalar_tensor_tensor(
                    out=xn[:, i, :],
                    in0=x_all[:, b, t0 + i, :],
                    scalar=rinv[:, g * GROUP + i : g * GROUP + i + 1],
                    in1=gamma_all[:],
                    op0=ALU.mult,
                    op1=ALU.mult,
                )
            xn_words = xn[:].bitcast(F32)
            pairs = []
            for h in range(GROUP // 2):
                xt = psum_t.tile([P, 2, 2, P], F32)
                for i in range(2):
                    for u in range(2):
                        nc.tensor.transpose(xt[:, i, u, :], xn_words[:, 2 * h + i, u * P : (u + 1) * P], ident[:])
                pairs.append(xt)
            transposed_of[g] = pairs

        def regroup(g):
            pairs = transposed_of.pop(g)
            grouped = work.tile([P, GROUP, P, PACK], BF16, align_bytes=64)
            grouped_words = grouped[:].bitcast(F32)
            for h in range(GROUP // 2):
                nc.scalar.copy(
                    out=grouped_words[:, 2 * h : 2 * h + 2, :, :], in_=pairs[h][:].rearrange("p i u r -> p i r u")
                )
            grouped_of[g] = grouped

        def quantise(g):
            grouped = grouped_of.pop(g)
            codes = work.tile([P, GROUP * P], U32, align_bytes=64)
            scales = work.tile([P, GROUP * P], U8, align_bytes=64)
            nc.vector.quantize_mx(
                out=codes[:].bitcast(FP8X4), scales=scales[:], in_=grouped[:].rearrange("p i r j -> p (i r j)")
            )
            operand_of[g] = (codes, scales)

        def project(g):
            codes, scales = operand_of.pop(g)
            v_bank = psum_v.tile([P, GROUP, INNER], F32)
            rot_banks = []
            for i in range(GROUP):
                rows = slice(i * P, (i + 1) * P)
                rot_bank = psum_rot.tile([P, ROT_COLS], F32)
                nc.tensor.matmul_mx(
                    out=rot_bank[:],
                    lhsT=codes[:, rows].bitcast(FP8X4),
                    lhsT_scale=scales[:, rows],
                    rhs=w_codes[:, 0:ROT_COLS].bitcast(FP8X4),
                    rhs_scale=w_scales[:, 0:ROT_COLS],
                    start=True,
                    stop=True,
                )
                nc.tensor.matmul_mx(
                    out=v_bank[:, i, :],
                    lhsT=codes[:, rows].bitcast(FP8X4),
                    lhsT_scale=scales[:, rows],
                    rhs=w_codes[:, ROT_COLS:].bitcast(FP8X4),
                    rhs_scale=w_scales[:, ROT_COLS:],
                    start=True,
                    stop=True,
                )
                rot_banks.append(rot_bank)
            banks_of[g] = rot_banks
            v_bank_of[g] = v_bank

        def copy_v(g):
            b, t0 = where(g)
            v_bank = v_bank_of.pop(g)
            v_out = results.tile([P, HEADS, GROUP, HEAD_DIM], F32)
            nc.scalar.copy(
                out=v_out[:].rearrange("p h i d -> p i h d"),
                in_=v_bank[:].rearrange("p i (h d) -> p i h d", h=HEADS),
            )
            nc.sync.dma_start(out=v_rows[b, :, :, t0 : t0 + GROUP, :], in_=v_out[:])

        def rotate(g):
            b, t0 = where(g)
            rot_banks = banks_of.pop(g)
            products = results.tile([P, GROUP, ROT_COLS], F32)
            for i in range(GROUP):
                factors = table[:, t0 + i, :, :, :].rearrange("p c q d -> p (c q) d").unsqueeze(2)
                nc.vector.tensor_tensor(
                    out=products[:, i, :].rearrange("p (c h d) -> p c h d", h=HEADS, d=HEAD_DIM),
                    in0=rot_banks[i][:].rearrange("p (c h d) -> p c h d", h=HEADS, d=HEAD_DIM),
                    in1=factors.to_broadcast([P, 4, HEADS, HEAD_DIM]),
                    op=ALU.mult,
                )
            products_of[g] = products

        def add_and_store(g):
            b, t0 = where(g)
            products = products_of.pop(g)
            qk_out = results.tile([P, 2 * HEADS, GROUP, HEAD_DIM], F32)
            adder = nc.vector if g == N_GROUPS - 1 else nc.gpsimd
            adder.tensor_tensor(
                out=qk_out[:].rearrange("p g i d -> p i g d"),
                in0=products[:, :, 0 : 2 * INNER].rearrange("p i (g d) -> p i g d", d=HEAD_DIM),
                in1=products[:, :, 2 * INNER :].rearrange("p i (g d) -> p i g d", d=HEAD_DIM),
                op=ALU.add,
            )
            nc.sync.dma_start(out=q_rows[b, :, :, t0 : t0 + GROUP, :], in_=qk_out[:, 0:HEADS, :, :])
            nc.sync.dma_start(out=k_rows[b, :, :, t0 : t0 + GROUP, :], in_=qk_out[:, HEADS:, :, :])

        def run(stage, g):
            if 0 <= g < N_GROUPS:
                stage(g)

        for g in range(-5, N_GROUPS + 1):
            run(project, g)
            run(normalise, g + 2)
            run(add_and_store, g - 1)
            run(sums, g + 5)
            run(copy_v, g)
            run(regroup, g + 2)
            run(fill_table, g + 2)
            run(rotate, g)
            run(quantise, g + 1)
